import numpy as np
import ml_dtypes

BF16 = ml_dtypes.bfloat16


def bf(x):
    return np.asarray(x, np.float32).astype(BF16)


def f32(x):
    return np.asarray(x, np.float32)


def f64(x):
    return np.asarray(x).astype(np.float64)


def striped(idx):
    return np.tile(idx.reshape(-1, 16).T, (8, 1))


C, S, N, L = 128, 4096, 1024, 4


def position_encoding():
    t = np.arange(1, L + 1, dtype=np.float64)[None, :]
    k = np.arange(1, C + 1, dtype=np.float64)[:, None]
    return 1.0 - t / L - (k / C) * (1.0 - 2.0 * t / L)


def setup_inputs():
    return {"base": f32(np.random.standard_normal((C, S))), "words": f32(np.random.standard_normal((C, L, N))), "pe": f32(position_encoding()), "ta": f32(np.random.standard_normal((C, N))), "offs": striped(np.random.permutation(S)[:N])}


def reference(base, words, pe, ta, offs):
    idx = offs[:16].T.reshape(-1)
    out = f64(base).copy()
    out[:, idx] = (f64(words) * f64(pe)[:, :, None]).sum(axis=1) + f64(ta)
    return out

@@ -1,0 +1,39 @@
+import concourse.mybir as mybir
+
+F32 = mybir.dt.float32
+U16 = mybir.dt.uint16
+MULT = mybir.AluOpType.mult
+ADD = mybir.AluOpType.add
+
+C = 128
+S = 4096
+N = 1024
+L = 4
+
+
+def tile_memn2n_ss_s_kernel(tc, base, words, pe, ta, offs, out):
+    nc = tc.nc
+    with tc.tile_pool(name="held", bufs=1) as held:
+        offsets = held.tile([C, N // 16], U16, name="offsets")
+        position = held.tile([C, L], F32, name="position")
+        word = held.tile([C, L, N], F32, name="word")
+        temporal = held.tile([C, N], F32, name="temporal")
+        memory = held.tile([C, S], F32, name="memory")
+        sentence = held.tile([C, N], F32, name="sentence")
+
+        nc.sync.dma_start(offsets[:], offs)
+        nc.sync.dma_start(position[:], pe)
+        for t in range(L):
+            nc.sync.dma_start(word[:, t, :], words[:, t, :])
+        nc.sync.dma_start(temporal[:], ta)
+        nc.sync.dma_start(memory[:], base)
+
+        nc.vector.tensor_scalar_mul(sentence[:], word[:, 0, :], position[:, 0:1])
+        for t in range(1, L):
+            nc.vector.scalar_tensor_tensor(
+                sentence[:], word[:, t, :], position[:, t : t + 1], sentence[:], MULT, ADD
+            )
+
+        nc.vector.tensor_tensor(memory[:].indirect(offsets[:]), sentence[:], temporal[:], ADD)
+
+        nc.sync.dma_start(out, memory[:])

@@ -23,8 +23,7 @@ def tile_memn2n_ss_s_kernel(tc, base, words, pe, ta, offs, out):
 
         nc.sync.dma_start(offsets[:], offs)
         nc.sync.dma_start(position[:], pe)
-        for t in range(L):
-            nc.sync.dma_start(word[:, t, :], words[:, t, :])
+        nc.sync.dma_start(word[:], words)
         nc.sync.dma_start(temporal[:], ta)
         nc.sync.dma_start(memory[:], base)
 

@@ -9,17 +9,18 @@ C = 128
 S = 4096
 N = 1024
 L = 4
+BIG = 4096
 
 
 def tile_memn2n_ss_s_kernel(tc, base, words, pe, ta, offs, out):
     nc = tc.nc
     with tc.tile_pool(name="held", bufs=1) as held:
+        memory = held.tile([C, S], F32, name="memory", align_bytes=BIG)
+        word = held.tile([C, L, N], F32, name="word", align_bytes=BIG)
+        temporal = held.tile([C, N], F32, name="temporal", align_bytes=BIG)
+        sentence = held.tile([C, N], F32, name="sentence")
         offsets = held.tile([C, N // 16], U16, name="offsets")
         position = held.tile([C, L], F32, name="position")
-        word = held.tile([C, L, N], F32, name="word")
-        temporal = held.tile([C, N], F32, name="temporal")
-        memory = held.tile([C, S], F32, name="memory")
-        sentence = held.tile([C, N], F32, name="sentence")
 
         nc.sync.dma_start(offsets[:], offs)
         nc.sync.dma_start(position[:], pe)

@@ -25,8 +25,8 @@ def tile_memn2n_ss_s_kernel(tc, base, words, pe, ta, offs, out):
         nc.sync.dma_start(offsets[:], offs)
         nc.sync.dma_start(position[:], pe)
         nc.sync.dma_start(word[:], words)
-        nc.sync.dma_start(temporal[:], ta)
         nc.sync.dma_start(memory[:], base)
+        nc.sync.dma_start(temporal[:], ta)
 
         nc.vector.tensor_scalar_mul(sentence[:], word[:, 0, :], position[:, 0:1])
         for t in range(1, L):

@@ -22,11 +22,11 @@ def tile_memn2n_ss_s_kernel(tc, base, words, pe, ta, offs, out):
         offsets = held.tile([C, N // 16], U16, name="offsets")
         position = held.tile([C, L], F32, name="position")
 
-        nc.sync.dma_start(offsets[:], offs)
-        nc.sync.dma_start(position[:], pe)
         nc.sync.dma_start(word[:], words)
+        nc.scalar.dma_start(position[:], pe)
+        nc.sync.dma_start(offsets[:], offs)
+        nc.scalar.dma_start(temporal[:], ta)
         nc.sync.dma_start(memory[:], base)
-        nc.sync.dma_start(temporal[:], ta)
 
         nc.vector.tensor_scalar_mul(sentence[:], word[:, 0, :], position[:, 0:1])
         for t in range(1, L):

import concourse.mybir as mybir

F32 = mybir.dt.float32
U16 = mybir.dt.uint16
MULT = mybir.AluOpType.mult
ADD = mybir.AluOpType.add

C = 128
S = 4096
N = 1024
L = 4
BIG = 4096


def tile_memn2n_ss_s_kernel(tc, base, words, pe, ta, offs, out):
    nc = tc.nc
    with tc.tile_pool(name="held", bufs=1) as held:
        memory = held.tile([C, S], F32, name="memory", align_bytes=BIG)
        word = held.tile([C, L, N], F32, name="word", align_bytes=BIG)
        temporal = held.tile([C, N], F32, name="temporal", align_bytes=BIG)
        sentence = held.tile([C, N], F32, name="sentence")
        offsets = held.tile([C, N // 16], U16, name="offsets")
        position = held.tile([C, L], F32, name="position")

        nc.sync.dma_start(word[:], words)
        nc.scalar.dma_start(position[:], pe)
        nc.sync.dma_start(offsets[:], offs)
        nc.scalar.dma_start(temporal[:], ta)
        nc.sync.dma_start(memory[:], base)

        nc.vector.tensor_scalar_mul(sentence[:], word[:, 0, :], position[:, 0:1])
        for t in range(1, L):
            nc.vector.scalar_tensor_tensor(
                sentence[:], word[:, t, :], position[:, t : t + 1], sentence[:], MULT, ADD
            )

        nc.vector.tensor_tensor(memory[:].indirect(offsets[:]), sentence[:], temporal[:], ADD)

        nc.sync.dma_start(out, memory[:])
